import numpy as np
import ml_dtypes


def mxq(x, axis, fmt="e4m3"):
    dtype, down = {"e4m3": (ml_dtypes.float8_e4m3fn, 7), "e5m2": (ml_dtypes.float8_e5m2, 14)}[fmt]
    v = np.moveaxis(np.asarray(x, np.float32).astype(ml_dtypes.bfloat16).astype(np.float64), axis, -1)
    blocks = v.reshape(v.shape[:-1] + (-1, 32))
    amax = np.abs(blocks).max(-1, keepdims=True)
    byte = np.maximum(np.where(amax > 0, np.frexp(amax)[1] - 1 + 127, 0) - down, 1)
    scale = np.exp2(byte - 127.0)
    codes = (blocks / scale).astype(np.float32).astype(dtype).astype(np.float64)
    return np.moveaxis((codes * scale).reshape(v.shape), -1, axis)


WIDE = False


def mx_kscale(k):
    if not WIDE:
        return np.ones(k)
    levels = np.array([10, -10, 5, -5, 0])
    a = np.random.permutation(np.resize(levels, k // 512 * 4)).reshape(k // 512, 4)
    idx = np.arange(k)
    return np.exp2(a[idx // 512, idx % 128 // 32])


BF16 = ml_dtypes.bfloat16


def bf(x):
    return np.asarray(x, np.float32).astype(BF16)


def f64(x):
    return np.asarray(x).astype(np.float64)


E2M1 = np.array([0.0, 0.5, 1.0, 1.5, 2.0, 3.0, 4.0, 6.0, -0.0, -0.5, -1.0, -1.5, -2.0, -3.0, -4.0, -6.0])


def pack_weight(w, fmt):
    k, n = w.shape
    w = f64(bf(w)).reshape(k // 32, 32, n)
    amax = np.abs(w).max(1)
    if fmt == "e4m3":
        byte = np.frexp(amax)[1] - 1 + 127 - 7
    else:
        mant, ex = np.frexp(amax / 6.0)
        byte = np.where(mant > 0.5, ex, ex - 1) + 127
    byte = np.clip(np.where(amax > 0, byte, 1), 1, 254)
    scaled = (w * np.exp2(127.0 - byte)[:, None, :]).reshape(k, n).astype(np.float32)
    by_word = np.ascontiguousarray(scaled.reshape(k // 512, 128, 4, n).transpose(0, 1, 3, 2))
    if fmt == "e4m3":
        words = by_word.astype(ml_dtypes.float8_e4m3fn).view(np.uint8)
    else:
        c = by_word.astype(ml_dtypes.float4_e2m1fn).view(np.uint8) & 0xF
        words = c[..., 0::2] | (c[..., 1::2] << 4)
    return np.ascontiguousarray(words), np.ascontiguousarray(byte.astype(np.uint8).reshape(k // 512, 16, n))


def unpack_weight(words, scales, fmt):
    g, p, n, _ = words.shape
    if fmt == "e4m3":
        vals = np.ascontiguousarray(words).view(ml_dtypes.float8_e4m3fn).astype(np.float64)
    else:
        nib = np.empty((g, p, n, 4), np.uint8)
        nib[..., 0::2] = words & 0xF
        nib[..., 1::2] = words >> 4
        vals = E2M1[nib]
    vals = vals * np.repeat(np.exp2(scales.astype(np.float64) - 127.0), 8, axis=1)[..., None]
    return vals.transpose(0, 1, 3, 2).reshape(g * 512, n)


N, IN_DIM, HID, OUT_DIM = 8192, 1024, 512, 128
CAT = 3 * HID


def log_softmax(v):
    d = v - v.max(-1, keepdims=True)
    return d - np.log(np.exp(d).sum(-1, keepdims=True))


def setup_inputs():
    s, t = mx_kscale(HID), mx_kscale(CAT)
    ta, tb, tc = t[:HID], t[HID:2 * HID], t[2 * HID:]
    u1 = bf(np.maximum(np.random.standard_normal((N, HID)) * 2.0, 0.0) * s)
    W2_1_words, W2_1_scales = pack_weight(np.random.standard_normal((HID, HID)) * 0.5 / np.sqrt(HID) / s[:, None] * tc, "e4m3")
    b2_1 = bf(np.random.standard_normal(HID) * 0.3 * tc)
    h = bf(np.random.standard_normal((N, HID)) * ta)
    h1 = bf(np.random.standard_normal((N, HID)) * 0.8 * tb)
    W_out_words, W_out_scales = pack_weight(np.random.standard_normal((CAT, OUT_DIM)) * 2.0 / np.sqrt(CAT) / t[:, None], "e4m3")
    b_out = bf(np.random.standard_normal(OUT_DIM) * 0.3)
    return {"u1": u1,
            "W2_1_words": W2_1_words,
            "W2_1_scales": W2_1_scales,
            "b2_1": b2_1,
            "h": h,
            "h1": h1,
            "W_out_words": W_out_words,
            "W_out_scales": W_out_scales,
            "b_out": b_out}


def reference(u1, W2_1_words, W2_1_scales, b2_1, h, h1, W_out_words, W_out_scales, b_out):
    h2 = (mxq(f64(u1), 1, "e4m3") @ unpack_weight(W2_1_words, W2_1_scales, "e4m3")) + f64(b2_1)
    cat = np.concatenate([f64(h), f64(h1), h2], axis=-1)
    logits = (mxq(cat, 1, "e4m3") @ unpack_weight(W_out_words, W_out_scales, "e4m3")) + f64(b_out)
    return log_softmax(logits)

@@ -1,0 +1,288 @@
+from contextlib import ExitStack
+
+import concourse.mybir as mybir
+from concourse.masks import make_identity
+
+F32 = mybir.dt.float32
+BF16 = mybir.dt.bfloat16
+I32 = mybir.dt.int32
+U32 = mybir.dt.uint32
+U8 = mybir.dt.uint8
+FP8X4 = mybir.dt.float8_e4m3fn_x4
+ALU = mybir.AluOpType
+ACT = mybir.ActivationFunctionType
+AXIS = mybir.AxisListType
+
+P = 128
+NODES = 8192
+HID = 512
+CLASSES = 128
+GROUPS = 3
+WORDS = HID // 2
+
+ROW_TILES = NODES // P
+R = 2
+ROUNDS = ROW_TILES // R
+ROUND_WIDTH = R * P * 4
+LOAD_TILES = 4
+LOAD_ROUNDS = LOAD_TILES // R
+CHUNKS = ROW_TILES // LOAD_TILES
+X_BUFS = 3
+
+BLOCK_ROUNDS = 16
+LAG_H2 = 1
+LAG_LOGITS = 2
+LAG_SOFTMAX = 3
+LAG_FINISH = LAG_SOFTMAX + BLOCK_ROUNDS
+
+FLOPS = 2 * NODES * HID * HID + 2 * NODES * GROUPS * HID * CLASSES
+
+
+def tile_gin_pc_t_kernel(
+    tc, u1, W2_1_words, W2_1_scales, b2_1, h, h1, W_out_words, W_out_scales, b_out, out
+):
+    nc = tc.nc
+    with ExitStack() as ctx:
+        ctx.enter_context(tc.manual_schedule())
+        consts = ctx.enter_context(tc.tile_pool(name="consts", bufs=1))
+        x_pool = ctx.enter_context(tc.tile_pool(name="x", bufs=X_BUFS))
+        work = ctx.enter_context(tc.tile_pool(name="work", bufs=2))
+        codes_pool = ctx.enter_context(tc.tile_pool(name="codes", bufs=3))
+        scratch = ctx.enter_context(tc.tile_pool(name="scratch", bufs=4))
+        turned_pool = ctx.enter_context(tc.psum_pool(name="turned", bufs=4))
+        h2_pool = ctx.enter_context(tc.psum_pool(name="h2", bufs=2))
+        logits_pool = ctx.enter_context(tc.psum_pool(name="logits", bufs=2))
+
+        u1_rows = u1.rearrange("(p i) k -> p i k", i=ROW_TILES)
+        h_rows = h.rearrange("(p i) k -> p i k", i=ROW_TILES)
+        h1_rows = h1.rearrange("(p i) k -> p i k", i=ROW_TILES)
+        out_rows = out.rearrange("(p i) c -> p i c", i=ROW_TILES)
+
+        def load_rows(rows, chunk, tag):
+            x_sb = x_pool.tile([P, LOAD_TILES, HID], BF16, tag=tag)
+            tiles = slice(chunk * LOAD_TILES, (chunk + 1) * LOAD_TILES)
+            nc.sync.dma_start(out=x_sb[:], in_=rows[:, tiles, :])
+            return x_sb
+
+        w21_scales = consts.tile([P, HID], U8, align_bytes=64)
+        wout_scales = consts.tile([P, GROUPS, CLASSES], U8, align_bytes=64)
+        nc.vector.memset(w21_scales[:].bitcast(I32), 0)
+        nc.vector.memset(wout_scales[:].bitcast(I32), 0)
+
+        ident = consts.tile([P, P], F32)
+        make_identity(nc, ident[:])
+
+        b21_sb = consts.tile([P, HID], BF16)
+        nc.scalar.dma_start(out=b21_sb[:], in_=b2_1.partition_broadcast(P))
+        bout_sb = consts.tile([P, CLASSES], BF16)
+        nc.scalar.dma_start(out=bout_sb[:], in_=b_out.partition_broadcast(P))
+
+        u1_sb, h_sb, h1_sb = {}, {}, {}
+        u1_sb[0] = load_rows(u1_rows, 0, "u1")
+        w21_words = consts.tile([P, HID], U32, align_bytes=64)
+        nc.sync.dma_start(
+            out=w21_words[:].bitcast(I32),
+            in_=W2_1_words[0].rearrange("p n t -> p (n t)").bitcast(I32),
+        )
+        for quadrant in range(4):
+            nc.sync.dma_start(
+                out=w21_scales[32 * quadrant : 32 * quadrant + 4, :].bitcast(I32),
+                in_=W2_1_scales[0, 4 * quadrant : 4 * quadrant + 4, :].bitcast(I32),
+            )
+        h_sb[0] = load_rows(h_rows, 0, "h")
+        h1_sb[0] = load_rows(h1_rows, 0, "h1")
+        wout_words = consts.tile([P, GROUPS, CLASSES], U32, align_bytes=64)
+        nc.sync.dma_start(
+            out=wout_words[:].bitcast(I32),
+            in_=W_out_words.rearrange("g p n t -> p g (n t)").bitcast(I32),
+        )
+        for quadrant in range(4):
+            nc.sync.dma_start(
+                out=wout_scales[32 * quadrant : 32 * quadrant + 4, :, :].bitcast(I32),
+                in_=W_out_scales[:, 4 * quadrant : 4 * quadrant + 4, :]
+                .rearrange("g r n -> r g n")
+                .bitcast(I32),
+            )
+
+        def load_chunk(chunk):
+            u1_sb[chunk] = load_rows(u1_rows, chunk, "u1")
+            h_sb[chunk] = load_rows(h_rows, chunk, "h")
+            h1_sb[chunk] = load_rows(h1_rows, chunk, "h1")
+
+        for chunk in range(1, X_BUFS):
+            load_chunk(chunk)
+
+        b21_sorted = consts.tile([P, HID], BF16)
+        nc.vector.tensor_copy(
+            out=b21_sorted[:].rearrange("p (u q e) -> p u q e", u=2, e=2),
+            in_=b21_sb[:].rearrange("p (q u e) -> p u q e", u=2, e=2),
+        )
+
+        z_all = consts.tile([P, ROW_TILES, CLASSES], F32)
+        neg_max = consts.tile([P, ROW_TILES], F32)
+        sum_exp = consts.tile([P, ROW_TILES], F32)
+        log_sum = consts.tile([P, ROW_TILES], F32)
+        neg_total = consts.tile([P, ROW_TILES], F32)
+
+        def turn(stationary):
+            bank = turned_pool.tile([P, R, 2, P], F32, tag="turned")
+            for r in range(R):
+                for u in range(2):
+                    nc.tensor.transpose(bank[:, r, u, :], stationary(r, u), ident[:])
+            return bank
+
+        def turn_input(x_sb, i):
+            words = x_sb[i // LOAD_ROUNDS][:].bitcast(F32)
+            first = (i % LOAD_ROUNDS) * R
+            return turn(lambda r, u: words[:, first + r, u:WORDS:2])
+
+        def regroup(bank, grouped):
+            nc.scalar.copy(
+                out=grouped.bitcast(F32).rearrange("p (r c u) -> p r c u", r=R, u=2),
+                in_=bank[:].rearrange("p r u c -> p r c u"),
+            )
+
+        def quantise(grouped, width, tag):
+            codes = codes_pool.tile([P, width // 4], U32, tag=tag + "_codes", align_bytes=64)
+            scales = codes_pool.tile([P, width // 4], U8, tag=tag + "_scales", align_bytes=64)
+            nc.vector.quantize_mx(out=codes[:].bitcast(FP8X4), scales=scales[:], in_=grouped)
+            return codes, scales
+
+        u1_grouped, hh_grouped, h2_grouped = {}, {}, {}
+        u1_mx, hh_mx, h2_mx = {}, {}, {}
+        h2_banks, h2_sorted, logits_bank = {}, {}, {}
+
+        def live(i):
+            return 0 <= i < ROUNDS
+
+        for step in range(ROUNDS + LAG_FINISH):
+            i = step
+            if step >= LOAD_ROUNDS and step % LOAD_ROUNDS == 0:
+                chunk = step // LOAD_ROUNDS + X_BUFS - 1
+                if chunk < CHUNKS:
+                    load_chunk(chunk)
+
+            j = step - LAG_H2
+            if live(j):
+                h2_sb = work.tile([P, R, HID], BF16, tag="h2_sorted")
+                for r in range(R):
+                    nc.vector.tensor_tensor(
+                        out=h2_sb[:, r, :].rearrange("p (u q e) -> p u q e", u=2, e=2),
+                        in0=h2_banks[j][r][:].rearrange("p (q u e) -> p u q e", u=2, e=2),
+                        in1=b21_sorted[:].rearrange("p (u q e) -> p u q e", u=2, e=2),
+                        op=ALU.add,
+                    )
+                h2_sorted[j] = h2_sb
+
+            if live(i):
+                g_u1 = work.tile([P, ROUND_WIDTH], BF16, tag="u1_grouped", align_bytes=64)
+                regroup(turn_input(u1_sb, i), g_u1[:])
+                u1_grouped[i] = g_u1
+                g_hh = work.tile([P, 2, ROUND_WIDTH], BF16, tag="hh_grouped", align_bytes=64)
+                regroup(turn_input(h_sb, i), g_hh[:, 0, :])
+                regroup(turn_input(h1_sb, i), g_hh[:, 1, :])
+                hh_grouped[i] = g_hh
+            if live(j):
+                h2_words = h2_sorted[j][:].bitcast(F32)
+                g_h2 = work.tile([P, ROUND_WIDTH], BF16, tag="h2_grouped", align_bytes=64)
+                regroup(turn(lambda r, u: h2_words[:, r, u * P : (u + 1) * P]), g_h2[:])
+                h2_grouped[j] = g_h2
+
+            s = step - LAG_SOFTMAX
+            tiles = slice(s * R, (s + 1) * R)
+            if live(i):
+                u1_mx[i] = quantise(u1_grouped[i][:], ROUND_WIDTH, "u1")
+            if live(s):
+                nc.vector.tensor_tensor(
+                    out=z_all[:, tiles, :],
+                    in0=logits_bank[s][:],
+                    in1=bout_sb[:].unsqueeze(1).to_broadcast([P, R, CLASSES]),
+                    op=ALU.add,
+                )
+            if live(j):
+                hh_mx[j] = quantise(
+                    hh_grouped[j][:].rearrange("p s w -> p (s w)"), 2 * ROUND_WIDTH, "hh"
+                )
+            if live(s):
+                nc.vector.tensor_reduce(
+                    out=neg_max[:, tiles], in_=z_all[:, tiles, :], axis=AXIS.X, op=ALU.max, negate=True
+                )
+            if live(j):
+                h2_mx[j] = quantise(h2_grouped[j][:], ROUND_WIDTH, "h2")
+
+            if live(i):
+                codes, scales = u1_mx[i]
+                h2_banks[i] = []
+                for r in range(R):
+                    nodes = slice(r * P, (r + 1) * P)
+                    h2_ps = h2_pool.tile([P, HID], F32, tag="h2_ps")
+                    nc.tensor.matmul_mx(
+                        out=h2_ps[:],
+                        lhsT=codes[:, nodes].bitcast(FP8X4),
+                        lhsT_scale=scales[:, nodes],
+                        rhs=w21_words[:].bitcast(FP8X4),
+                        rhs_scale=w21_scales[:],
+                        start=True,
+                        stop=True,
+                    )
+                    h2_banks[i].append(h2_ps)
+            m = step - LAG_LOGITS
+            if live(m):
+                logits_ps = logits_pool.tile([P, R, CLASSES], F32, tag="logits_ps")
+                for r in range(R):
+                    operands = (
+                        (hh_mx[m], r * P),
+                        (hh_mx[m], (R + r) * P),
+                        (h2_mx[m], r * P),
+                    )
+                    for g in range(GROUPS):
+                        (codes, scales), first = operands[g]
+                        nodes = slice(first, first + P)
+                        nc.tensor.matmul_mx(
+                            out=logits_ps[:, r, :],
+                            lhsT=codes[:, nodes].bitcast(FP8X4),
+                            lhsT_scale=scales[:, nodes],
+                            rhs=wout_words[:, g, :].bitcast(FP8X4),
+                            rhs_scale=wout_scales[:, g, :],
+                            start=(g == 0),
+                            stop=(g == GROUPS - 1),
+                        )
+                logits_bank[m] = logits_ps
+
+            if live(s):
+                for t in range(s * R, (s + 1) * R):
+                    exp_sb = scratch.tile([P, CLASSES], F32, tag="exp")
+                    nc.scalar.activation(
+                        out=exp_sb[:],
+                        in_=z_all[:, t, :],
+                        func=ACT.Exp,
+                        bias=neg_max[:, t : t + 1],
+                        scale=1.0,
+                        accum_out=sum_exp[:, t : t + 1],
+                    )
+                if (s + 1) % BLOCK_ROUNDS == 0:
+                    block = slice((s + 1 - BLOCK_ROUNDS) * R, (s + 1) * R)
+                    nc.scalar.activation(out=log_sum[:, block], in_=sum_exp[:, block], func=ACT.Ln)
+                    nc.vector.tensor_tensor(
+                        out=neg_total[:, block],
+                        in0=neg_max[:, block],
+                        in1=log_sum[:, block],
+                        op=ALU.subtract,
+                    )
+
+            f = step - LAG_FINISH
+            if live(f):
+                t = f * R
+                nc.scalar.activation(
+                    out=z_all[:, t, :],
+                    in_=z_all[:, t, :],
+                    func=ACT.Identity,
+                    bias=neg_total[:, t : t + 1],
+                    scale=1.0,
+                )
+                nc.vector.tensor_scalar_add(
+                    out=z_all[:, t + 1, :], in0=z_all[:, t + 1, :], scalar1=neg_total[:, t + 1 : t + 2]
+                )
+                if (f + 1) % LOAD_ROUNDS == 0:
+                    done = slice((f + 1) * R - LOAD_TILES, (f + 1) * R)
+                    nc.sync.dma_start(out=out_rows[:, done, :], in_=z_all[:, done, :])

@@ -32,8 +32,9 @@ X_BUFS = 3
 BLOCK_ROUNDS = 16
 LAG_H2 = 1
 LAG_LOGITS = 2
-LAG_SOFTMAX = 3
-LAG_FINISH = LAG_SOFTMAX + BLOCK_ROUNDS
+LAG_MAXIMUM = 3
+LAG_EXP = 4
+LAG_FINISH = LAG_EXP + BLOCK_ROUNDS
 
 FLOPS = 2 * NODES * HID * HID + 2 * NODES * GROUPS * HID * CLASSES
 
@@ -152,137 +153,161 @@ def tile_gin_pc_t_kernel(
         u1_mx, hh_mx, h2_mx = {}, {}, {}
         h2_banks, h2_sorted, logits_bank = {}, {}, {}
 
-        def live(i):
-            return 0 <= i < ROUNDS
+        def turn_u1_and_h(i):
+            g_u1 = work.tile([P, ROUND_WIDTH], BF16, tag="u1_grouped", align_bytes=64)
+            regroup(turn_input(u1_sb, i), g_u1[:])
+            u1_grouped[i] = g_u1
+            g_hh = work.tile([P, 2, ROUND_WIDTH], BF16, tag="hh_grouped", align_bytes=64)
+            regroup(turn_input(h_sb, i), g_hh[:, 0, :])
+            hh_grouped[i] = g_hh
 
-        for step in range(ROUNDS + LAG_FINISH):
-            i = step
-            if step >= LOAD_ROUNDS and step % LOAD_ROUNDS == 0:
-                chunk = step // LOAD_ROUNDS + X_BUFS - 1
-                if chunk < CHUNKS:
-                    load_chunk(chunk)
+        def turn_h1(i):
+            regroup(turn_input(h1_sb, i), hh_grouped[i][:, 1, :])
 
-            j = step - LAG_H2
-            if live(j):
-                h2_sb = work.tile([P, R, HID], BF16, tag="h2_sorted")
-                for r in range(R):
-                    nc.vector.tensor_tensor(
-                        out=h2_sb[:, r, :].rearrange("p (u q e) -> p u q e", u=2, e=2),
-                        in0=h2_banks[j][r][:].rearrange("p (q u e) -> p u q e", u=2, e=2),
-                        in1=b21_sorted[:].rearrange("p (u q e) -> p u q e", u=2, e=2),
-                        op=ALU.add,
-                    )
-                h2_sorted[j] = h2_sb
+        def quantise_u1(i):
+            u1_mx[i] = quantise(u1_grouped[i][:], ROUND_WIDTH, "u1")
 
-            if live(i):
-                g_u1 = work.tile([P, ROUND_WIDTH], BF16, tag="u1_grouped", align_bytes=64)
-                regroup(turn_input(u1_sb, i), g_u1[:])
-                u1_grouped[i] = g_u1
-                g_hh = work.tile([P, 2, ROUND_WIDTH], BF16, tag="hh_grouped", align_bytes=64)
-                regroup(turn_input(h_sb, i), g_hh[:, 0, :])
-                regroup(turn_input(h1_sb, i), g_hh[:, 1, :])
-                hh_grouped[i] = g_hh
-            if live(j):
-                h2_words = h2_sorted[j][:].bitcast(F32)
-                g_h2 = work.tile([P, ROUND_WIDTH], BF16, tag="h2_grouped", align_bytes=64)
-                regroup(turn(lambda r, u: h2_words[:, r, u * P : (u + 1) * P]), g_h2[:])
-                h2_grouped[j] = g_h2
+        def quantise_h_and_h1(i):
+            hh_mx[i] = quantise(
+                hh_grouped[i][:].rearrange("p s w -> p (s w)"), 2 * ROUND_WIDTH, "hh"
+            )
 
-            s = step - LAG_SOFTMAX
-            tiles = slice(s * R, (s + 1) * R)
-            if live(i):
-                u1_mx[i] = quantise(u1_grouped[i][:], ROUND_WIDTH, "u1")
-            if live(s):
+        def first_matmul(i):
+            codes, scales = u1_mx[i]
+            h2_banks[i] = []
+            for r in range(R):
+                nodes = slice(r * P, (r + 1) * P)
+                h2_ps = h2_pool.tile([P, HID], F32, tag="h2_ps")
+                nc.tensor.matmul_mx(
+                    out=h2_ps[:],
+                    lhsT=codes[:, nodes].bitcast(FP8X4),
+                    lhsT_scale=scales[:, nodes],
+                    rhs=w21_words[:].bitcast(FP8X4),
+                    rhs_scale=w21_scales[:],
+                    start=True,
+                    stop=True,
+                )
+                h2_banks[i].append(h2_ps)
+
+        def add_b2_1(i):
+            h2_sb = work.tile([P, R, HID], BF16, tag="h2_sorted")
+            for r in range(R):
                 nc.vector.tensor_tensor(
-                    out=z_all[:, tiles, :],
-                    in0=logits_bank[s][:],
-                    in1=bout_sb[:].unsqueeze(1).to_broadcast([P, R, CLASSES]),
+                    out=h2_sb[:, r, :].rearrange("p (u q e) -> p u q e", u=2, e=2),
+                    in0=h2_banks[i][r][:].rearrange("p (q u e) -> p u q e", u=2, e=2),
+                    in1=b21_sorted[:].rearrange("p (u q e) -> p u q e", u=2, e=2),
                     op=ALU.add,
                 )
-            if live(j):
-                hh_mx[j] = quantise(
-                    hh_grouped[j][:].rearrange("p s w -> p (s w)"), 2 * ROUND_WIDTH, "hh"
-                )
-            if live(s):
-                nc.vector.tensor_reduce(
-                    out=neg_max[:, tiles], in_=z_all[:, tiles, :], axis=AXIS.X, op=ALU.max, negate=True
-                )
-            if live(j):
-                h2_mx[j] = quantise(h2_grouped[j][:], ROUND_WIDTH, "h2")
+            h2_sorted[i] = h2_sb
 
-            if live(i):
-                codes, scales = u1_mx[i]
-                h2_banks[i] = []
-                for r in range(R):
-                    nodes = slice(r * P, (r + 1) * P)
-                    h2_ps = h2_pool.tile([P, HID], F32, tag="h2_ps")
+        def turn_h2(i):
+            h2_words = h2_sorted[i][:].bitcast(F32)
+            g_h2 = work.tile([P, ROUND_WIDTH], BF16, tag="h2_grouped", align_bytes=64)
+            regroup(turn(lambda r, u: h2_words[:, r, u * P : (u + 1) * P]), g_h2[:])
+            h2_grouped[i] = g_h2
+
+        def quantise_h2(i):
+            h2_mx[i] = quantise(h2_grouped[i][:], ROUND_WIDTH, "h2")
+
+        def second_matmul(i):
+            logits_ps = logits_pool.tile([P, R, CLASSES], F32, tag="logits_ps")
+            for r in range(R):
+                operands = ((hh_mx[i], r * P), (hh_mx[i], (R + r) * P), (h2_mx[i], r * P))
+                for g in range(GROUPS):
+                    (codes, scales), first = operands[g]
+                    nodes = slice(first, first + P)
                     nc.tensor.matmul_mx(
-                        out=h2_ps[:],
+                        out=logits_ps[:, r, :],
                         lhsT=codes[:, nodes].bitcast(FP8X4),
                         lhsT_scale=scales[:, nodes],
-                        rhs=w21_words[:].bitcast(FP8X4),
-                        rhs_scale=w21_scales[:],
-                        start=True,
-                        stop=True,
+                        rhs=wout_words[:, g, :].bitcast(FP8X4),
+                        rhs_scale=wout_scales[:, g, :],
+                        start=(g == 0),
+                        stop=(g == GROUPS - 1),
                     )
-                    h2_banks[i].append(h2_ps)
-            m = step - LAG_LOGITS
-            if live(m):
-                logits_ps = logits_pool.tile([P, R, CLASSES], F32, tag="logits_ps")
-                for r in range(R):
-                    operands = (
-                        (hh_mx[m], r * P),
-                        (hh_mx[m], (R + r) * P),
-                        (h2_mx[m], r * P),
-                    )
-                    for g in range(GROUPS):
-                        (codes, scales), first = operands[g]
-                        nodes = slice(first, first + P)
-                        nc.tensor.matmul_mx(
-                            out=logits_ps[:, r, :],
-                            lhsT=codes[:, nodes].bitcast(FP8X4),
-                            lhsT_scale=scales[:, nodes],
-                            rhs=wout_words[:, g, :].bitcast(FP8X4),
-                            rhs_scale=wout_scales[:, g, :],
-                            start=(g == 0),
-                            stop=(g == GROUPS - 1),
-                        )
-                logits_bank[m] = logits_ps
+            logits_bank[i] = logits_ps
 
-            if live(s):
-                for t in range(s * R, (s + 1) * R):
-                    exp_sb = scratch.tile([P, CLASSES], F32, tag="exp")
-                    nc.scalar.activation(
-                        out=exp_sb[:],
-                        in_=z_all[:, t, :],
-                        func=ACT.Exp,
-                        bias=neg_max[:, t : t + 1],
-                        scale=1.0,
-                        accum_out=sum_exp[:, t : t + 1],
-                    )
-                if (s + 1) % BLOCK_ROUNDS == 0:
-                    block = slice((s + 1 - BLOCK_ROUNDS) * R, (s + 1) * R)
-                    nc.scalar.activation(out=log_sum[:, block], in_=sum_exp[:, block], func=ACT.Ln)
-                    nc.vector.tensor_tensor(
-                        out=neg_total[:, block],
-                        in0=neg_max[:, block],
-                        in1=log_sum[:, block],
-                        op=ALU.subtract,
-                    )
+        def add_b_out(i):
+            nc.vector.tensor_tensor(
+                out=z_all[:, i * R : (i + 1) * R, :],
+                in0=logits_bank[i][:],
+                in1=bout_sb[:].unsqueeze(1).to_broadcast([P, R, CLASSES]),
+                op=ALU.add,
+            )
 
-            f = step - LAG_FINISH
-            if live(f):
-                t = f * R
+        def row_maximum(i):
+            tiles = slice(i * R, (i + 1) * R)
+            nc.vector.tensor_reduce(
+                out=neg_max[:, tiles], in_=z_all[:, tiles, :], axis=AXIS.X, op=ALU.max, negate=True
+            )
+
+        def exponentials(i):
+            for t in range(i * R, (i + 1) * R):
+                exp_sb = scratch.tile([P, CLASSES], F32, tag="exp")
                 nc.scalar.activation(
-                    out=z_all[:, t, :],
+                    out=exp_sb[:],
                     in_=z_all[:, t, :],
-                    func=ACT.Identity,
-                    bias=neg_total[:, t : t + 1],
+                    func=ACT.Exp,
+                    bias=neg_max[:, t : t + 1],
                     scale=1.0,
+                    accum_out=sum_exp[:, t : t + 1],
                 )
-                nc.vector.tensor_scalar_add(
-                    out=z_all[:, t + 1, :], in0=z_all[:, t + 1, :], scalar1=neg_total[:, t + 1 : t + 2]
+            if (i + 1) % BLOCK_ROUNDS == 0:
+                block = slice((i + 1 - BLOCK_ROUNDS) * R, (i + 1) * R)
+                nc.scalar.activation(out=log_sum[:, block], in_=sum_exp[:, block], func=ACT.Ln)
+
+        def block_total(i):
+            if (i + 1) % BLOCK_ROUNDS == 0:
+                block = slice((i + 1 - BLOCK_ROUNDS) * R, (i + 1) * R)
+                nc.vector.tensor_tensor(
+                    out=neg_total[:, block],
+                    in0=neg_max[:, block],
+                    in1=log_sum[:, block],
+                    op=ALU.subtract,
                 )
-                if (f + 1) % LOAD_ROUNDS == 0:
-                    done = slice((f + 1) * R - LOAD_TILES, (f + 1) * R)
-                    nc.sync.dma_start(out=out_rows[:, done, :], in_=z_all[:, done, :])
+
+        def finish_first_tile(i):
+            t = i * R
+            nc.scalar.activation(
+                out=z_all[:, t, :],
+                in_=z_all[:, t, :],
+                func=ACT.Identity,
+                bias=neg_total[:, t : t + 1],
+                scale=1.0,
+            )
+
+        def finish_second_tile_and_store(i):
+            t = i * R + 1
+            nc.vector.tensor_scalar_add(
+                out=z_all[:, t, :], in0=z_all[:, t, :], scalar1=neg_total[:, t : t + 1]
+            )
+            if (i + 1) % LOAD_ROUNDS == 0:
+                done = slice((i + 1) * R - LOAD_TILES, (i + 1) * R)
+                nc.sync.dma_start(out=out_rows[:, done, :], in_=z_all[:, done, :])
+
+        def prefetch(step):
+            chunk = step // LOAD_ROUNDS + X_BUFS - 1
+            if step >= LOAD_ROUNDS and step % LOAD_ROUNDS == 0 and chunk < CHUNKS:
+                load_chunk(chunk)
+
+        def if_live(stage, i):
+            if 0 <= i < ROUNDS:
+                stage(i)
+
+        for step in range(ROUNDS + LAG_FINISH):
+            prefetch(step)
+            if_live(quantise_h2, step - LAG_LOGITS)
+            if_live(add_b2_1, step - LAG_H2)
+            if_live(turn_u1_and_h, step)
+            if_live(second_matmul, step - LAG_LOGITS)
+            if_live(exponentials, step - LAG_EXP)
+            if_live(finish_first_tile, step - LAG_FINISH)
+            if_live(turn_h1, step)
+            if_live(turn_h2, step - LAG_H2)
+            if_live(quantise_u1, step)
+            if_live(first_matmul, step)
+            if_live(add_b_out, step - LAG_MAXIMUM)
+            if_live(quantise_h_and_h1, step - LAG_H2)
+            if_live(row_maximum, step - LAG_MAXIMUM)
+            if_live(block_total, step - LAG_EXP)
+            if_live(finish_second_tile_and_store, step - LAG_FINISH)

@@ -18,23 +18,27 @@ NODES = 8192
 HID = 512
 CLASSES = 128
 GROUPS = 3
+PACK = 4
 WORDS = HID // 2
 
 ROW_TILES = NODES // P
 R = 2
-ROUNDS = ROW_TILES // R
-ROUND_WIDTH = R * P * 4
+UNITS = ROW_TILES // R
+UNIT_WIDTH = R * P * PACK
+UNIT_CODES = R * P
 LOAD_TILES = 4
-LOAD_ROUNDS = LOAD_TILES // R
+LOAD_UNITS = LOAD_TILES // R
 CHUNKS = ROW_TILES // LOAD_TILES
-X_BUFS = 3
+X_BUFS = 4
 
-BLOCK_ROUNDS = 16
-LAG_H2 = 1
-LAG_LOGITS = 2
-LAG_MAXIMUM = 3
-LAG_EXP = 4
-LAG_FINISH = LAG_EXP + BLOCK_ROUNDS
+BLOCK_ENDS = (16, 28, 32)
+FIN_PER_STEP = 3
+
+LEAD_TU = 3
+LEAD_TH = 2
+LAG_MM2 = 1
+LAG_Z = 2
+LAG_EXP = 3
 
 FLOPS = 2 * NODES * HID * HID + 2 * NODES * GROUPS * HID * CLASSES
 
@@ -47,7 +51,7 @@ def tile_gin_pc_t_kernel(
         ctx.enter_context(tc.manual_schedule())
         consts = ctx.enter_context(tc.tile_pool(name="consts", bufs=1))
         x_pool = ctx.enter_context(tc.tile_pool(name="x", bufs=X_BUFS))
-        work = ctx.enter_context(tc.tile_pool(name="work", bufs=2))
+        grouped_pool = ctx.enter_context(tc.tile_pool(name="grouped", bufs=4))
         codes_pool = ctx.enter_context(tc.tile_pool(name="codes", bufs=3))
         scratch = ctx.enter_context(tc.tile_pool(name="scratch", bufs=4))
         turned_pool = ctx.enter_context(tc.psum_pool(name="turned", bufs=4))
@@ -59,39 +63,45 @@ def tile_gin_pc_t_kernel(
         h1_rows = h1.rearrange("(p i) k -> p i k", i=ROW_TILES)
         out_rows = out.rearrange("(p i) c -> p i c", i=ROW_TILES)
 
-        def load_rows(rows, chunk, tag):
-            x_sb = x_pool.tile([P, LOAD_TILES, HID], BF16, tag=tag)
-            tiles = slice(chunk * LOAD_TILES, (chunk + 1) * LOAD_TILES)
-            nc.sync.dma_start(out=x_sb[:], in_=rows[:, tiles, :])
-            return x_sb
+        u1_sb, h_sb, h1_sb = {}, {}, {}
 
-        w21_scales = consts.tile([P, HID], U8, align_bytes=64)
+        def load_rows(rows, store, chunk, tag, pieces=1):
+            x_sb = x_pool.tile([P, LOAD_TILES, HID], BF16, tag=tag)
+            step = LOAD_TILES // pieces
+            for piece in range(pieces):
+                lo = piece * step
+                nc.sync.dma_start(
+                    out=x_sb[:, lo : lo + step, :],
+                    in_=rows[:, chunk * LOAD_TILES + lo : chunk * LOAD_TILES + lo + step, :],
+                )
+            store[chunk] = x_sb
+
+        w21_scales_raw = consts.tile([P, HID], U8, align_bytes=64)
         wout_scales = consts.tile([P, GROUPS, CLASSES], U8, align_bytes=64)
-        nc.vector.memset(w21_scales[:].bitcast(I32), 0)
+        nc.vector.memset(w21_scales_raw[:].bitcast(I32), 0)
         nc.vector.memset(wout_scales[:].bitcast(I32), 0)
 
         ident = consts.tile([P, P], F32)
         make_identity(nc, ident[:])
 
-        b21_sb = consts.tile([P, HID], BF16)
-        nc.scalar.dma_start(out=b21_sb[:], in_=b2_1.partition_broadcast(P))
+        b21_sb = consts.tile([P, PACK], BF16)
+        nc.scalar.dma_start(out=b21_sb[:], in_=b2_1.rearrange("(p t) -> p t", t=PACK))
         bout_sb = consts.tile([P, CLASSES], BF16)
         nc.scalar.dma_start(out=bout_sb[:], in_=b_out.partition_broadcast(P))
 
-        u1_sb, h_sb, h1_sb = {}, {}, {}
-        u1_sb[0] = load_rows(u1_rows, 0, "u1")
-        w21_words = consts.tile([P, HID], U32, align_bytes=64)
+        load_rows(u1_rows, u1_sb, 0, "u1", pieces=2)
+        w21_words_raw = consts.tile([P, HID], U32, align_bytes=64)
         nc.sync.dma_start(
-            out=w21_words[:].bitcast(I32),
+            out=w21_words_raw[:].bitcast(I32),
             in_=W2_1_words[0].rearrange("p n t -> p (n t)").bitcast(I32),
         )
         for quadrant in range(4):
             nc.sync.dma_start(
-                out=w21_scales[32 * quadrant : 32 * quadrant + 4, :].bitcast(I32),
+                out=w21_scales_raw[32 * quadrant : 32 * quadrant + 4, :].bitcast(I32),
                 in_=W2_1_scales[0, 4 * quadrant : 4 * quadrant + 4, :].bitcast(I32),
             )
-        h_sb[0] = load_rows(h_rows, 0, "h")
-        h1_sb[0] = load_rows(h1_rows, 0, "h1")
+        load_rows(h_rows, h_sb, 0, "h", pieces=2)
+        load_rows(h1_rows, h1_sb, 0, "h1", pieces=2)
         wout_words = consts.tile([P, GROUPS, CLASSES], U32, align_bytes=64)
         nc.sync.dma_start(
             out=wout_words[:].bitcast(I32),
@@ -104,20 +114,21 @@ def tile_gin_pc_t_kernel(
                 .rearrange("g r n -> r g n")
                 .bitcast(I32),
             )
-
-        def load_chunk(chunk):
-            u1_sb[chunk] = load_rows(u1_rows, chunk, "u1")
-            h_sb[chunk] = load_rows(h_rows, chunk, "h")
-            h1_sb[chunk] = load_rows(h1_rows, chunk, "h1")
-
         for chunk in range(1, X_BUFS):
-            load_chunk(chunk)
+            load_rows(u1_rows, u1_sb, chunk, "u1")
+            load_rows(h_rows, h_sb, chunk, "h")
+            load_rows(h1_rows, h1_sb, chunk, "h1")
 
-        b21_sorted = consts.tile([P, HID], BF16)
+        w21_words = consts.tile([P, HID], U32, align_bytes=64)
         nc.vector.tensor_copy(
-            out=b21_sorted[:].rearrange("p (u q e) -> p u q e", u=2, e=2),
-            in_=b21_sb[:].rearrange("p (q u e) -> p u q e", u=2, e=2),
+            out=w21_words[:].bitcast(I32).rearrange("p (t m) -> p t m", t=PACK),
+            in_=w21_words_raw[:].bitcast(I32).rearrange("p (m t) -> p t m", t=PACK),
         )
+        w21_scales = consts.tile([P, HID], U8, align_bytes=64)
+        for t in range(PACK):
+            nc.vector.tensor_copy(
+                out=w21_scales[:, t * P : (t + 1) * P], in_=w21_scales_raw[:, t:HID:PACK]
+            )
 
         z_all = consts.tile([P, ROW_TILES, CLASSES], F32)
         neg_max = consts.tile([P, ROW_TILES], F32)
@@ -125,94 +136,107 @@ def tile_gin_pc_t_kernel(
         log_sum = consts.tile([P, ROW_TILES], F32)
         neg_total = consts.tile([P, ROW_TILES], F32)
 
-        def turn(stationary):
+        uq_grouped, hh_grouped = {}, {}
+        uq_mx, hh_mx = {}, {}
+        h2_banks, logits_bank = {}, {}
+
+        def uq_tile(j):
+            if j not in uq_grouped:
+                uq_grouped[j] = grouped_pool.tile(
+                    [P, 2, UNIT_WIDTH], BF16, tag="uq_grouped", align_bytes=64, name="uq_g"
+                )
+            return uq_grouped[j]
+
+        def turn_and_regroup(x_sb, j, grouped):
+            words = x_sb[j // LOAD_UNITS][:].bitcast(F32)
+            first = (j % LOAD_UNITS) * R
             bank = turned_pool.tile([P, R, 2, P], F32, tag="turned")
             for r in range(R):
                 for u in range(2):
-                    nc.tensor.transpose(bank[:, r, u, :], stationary(r, u), ident[:])
-            return bank
-
-        def turn_input(x_sb, i):
-            words = x_sb[i // LOAD_ROUNDS][:].bitcast(F32)
-            first = (i % LOAD_ROUNDS) * R
-            return turn(lambda r, u: words[:, first + r, u:WORDS:2])
-
-        def regroup(bank, grouped):
+                    nc.tensor.transpose(bank[:, r, u, :], words[:, first + r, u:WORDS:2], ident[:])
             nc.scalar.copy(
                 out=grouped.bitcast(F32).rearrange("p (r c u) -> p r c u", r=R, u=2),
                 in_=bank[:].rearrange("p r u c -> p r c u"),
             )
 
-        def quantise(grouped, width, tag):
-            codes = codes_pool.tile([P, width // 4], U32, tag=tag + "_codes", align_bytes=64)
-            scales = codes_pool.tile([P, width // 4], U8, tag=tag + "_scales", align_bytes=64)
-            nc.vector.quantize_mx(out=codes[:].bitcast(FP8X4), scales=scales[:], in_=grouped)
-            return codes, scales
+        def refill(rows, store, j, tag):
+            chunk = j // LOAD_UNITS + X_BUFS
+            if j % LOAD_UNITS == LOAD_UNITS - 1 and chunk < CHUNKS:
+                load_rows(rows, store, chunk, tag)
 
-        u1_grouped, hh_grouped, h2_grouped = {}, {}, {}
-        u1_mx, hh_mx, h2_mx = {}, {}, {}
-        h2_banks, h2_sorted, logits_bank = {}, {}, {}
+        def turn_u1(j):
+            turn_and_regroup(u1_sb, j, uq_tile(j - 1)[:, 0, :])
+            refill(u1_rows, u1_sb, j, "u1")
 
-        def turn_u1_and_h(i):
-            g_u1 = work.tile([P, ROUND_WIDTH], BF16, tag="u1_grouped", align_bytes=64)
-            regroup(turn_input(u1_sb, i), g_u1[:])
-            u1_grouped[i] = g_u1
-            g_hh = work.tile([P, 2, ROUND_WIDTH], BF16, tag="hh_grouped", align_bytes=64)
-            regroup(turn_input(h_sb, i), g_hh[:, 0, :])
-            hh_grouped[i] = g_hh
+        def turn_h_and_h1(j):
+            g_hh = grouped_pool.tile([P, 2, UNIT_WIDTH], BF16, tag="hh_grouped", align_bytes=64)
+            hh_grouped[j] = g_hh
+            turn_and_regroup(h_sb, j, g_hh[:, 0, :])
+            refill(h_rows, h_sb, j, "h")
+            turn_and_regroup(h1_sb, j, g_hh[:, 1, :])
+            refill(h1_rows, h1_sb, j, "h1")
 
-        def turn_h1(i):
-            regroup(turn_input(h1_sb, i), hh_grouped[i][:, 1, :])
-
-        def quantise_u1(i):
-            u1_mx[i] = quantise(u1_grouped[i][:], ROUND_WIDTH, "u1")
-
-        def quantise_h_and_h1(i):
-            hh_mx[i] = quantise(
-                hh_grouped[i][:].rearrange("p s w -> p (s w)"), 2 * ROUND_WIDTH, "hh"
+        def quantise_uq(j):
+            codes = codes_pool.tile([P, 2 * UNIT_CODES], U32, tag="uq_codes", align_bytes=64)
+            scales = codes_pool.tile([P, 2 * UNIT_CODES], U8, tag="uq_scales", align_bytes=64)
+            lo = 0 if j + 1 < UNITS else 1
+            hi = 2 if j >= 0 else 1
+            nc.vector.quantize_mx(
+                out=codes[:, lo * UNIT_CODES : hi * UNIT_CODES].bitcast(FP8X4),
+                scales=scales[:, lo * UNIT_CODES : hi * UNIT_CODES],
+                in_=uq_tile(j)[:, lo:hi, :].rearrange("p s w -> p (s w)"),
             )
+            uq_mx[j] = (codes, scales)
 
-        def first_matmul(i):
-            codes, scales = u1_mx[i]
-            h2_banks[i] = []
+        def quantise_hh(j):
+            codes = codes_pool.tile([P, 2 * UNIT_CODES], U32, tag="hh_codes", align_bytes=64)
+            scales = codes_pool.tile([P, 2 * UNIT_CODES], U8, tag="hh_scales", align_bytes=64)
+            nc.vector.quantize_mx(
+                out=codes[:].bitcast(FP8X4),
+                scales=scales[:],
+                in_=hh_grouped[j][:].rearrange("p s w -> p (s w)"),
+            )
+            hh_mx[j] = (codes, scales)
+
+        def first_matmul(j):
+            codes, scales = uq_mx[j - 1]
+            h2_banks[j] = []
             for r in range(R):
                 nodes = slice(r * P, (r + 1) * P)
-                h2_ps = h2_pool.tile([P, HID], F32, tag="h2_ps")
-                nc.tensor.matmul_mx(
-                    out=h2_ps[:],
-                    lhsT=codes[:, nodes].bitcast(FP8X4),
-                    lhsT_scale=scales[:, nodes],
-                    rhs=w21_words[:].bitcast(FP8X4),
-                    rhs_scale=w21_scales[:],
-                    start=True,
-                    stop=True,
-                )
-                h2_banks[i].append(h2_ps)
+                h2_ps = h2_pool.tile([P, PACK, P], F32, tag="h2_ps")
+                for t in range(PACK):
+                    channels = slice(t * P, (t + 1) * P)
+                    nc.tensor.matmul_mx(
+                        out=h2_ps[:, t, :],
+                        lhsT=w21_words[:, channels].bitcast(FP8X4),
+                        lhsT_scale=w21_scales[:, channels],
+                        rhs=codes[:, nodes].bitcast(FP8X4),
+                        rhs_scale=scales[:, nodes],
+                        start=True,
+                        stop=True,
+                    )
+                h2_banks[j].append(h2_ps)
 
-        def add_b2_1(i):
-            h2_sb = work.tile([P, R, HID], BF16, tag="h2_sorted")
+        def add_b2_1(j):
+            g = uq_tile(j)
             for r in range(R):
                 nc.vector.tensor_tensor(
-                    out=h2_sb[:, r, :].rearrange("p (u q e) -> p u q e", u=2, e=2),
-                    in0=h2_banks[i][r][:].rearrange("p (q u e) -> p u q e", u=2, e=2),
-                    in1=b21_sorted[:].rearrange("p (u q e) -> p u q e", u=2, e=2),
+                    out=g[:, 1, r * P * PACK : (r + 1) * P * PACK].rearrange(
+                        "p (c t) -> p c t", t=PACK
+                    ),
+                    in0=h2_banks[j][r][:].rearrange("p t c -> p c t"),
+                    in1=b21_sb[:].unsqueeze(1).to_broadcast([P, P, PACK]),
                     op=ALU.add,
                 )
-            h2_sorted[i] = h2_sb
 
-        def turn_h2(i):
-            h2_words = h2_sorted[i][:].bitcast(F32)
-            g_h2 = work.tile([P, ROUND_WIDTH], BF16, tag="h2_grouped", align_bytes=64)
-            regroup(turn(lambda r, u: h2_words[:, r, u * P : (u + 1) * P]), g_h2[:])
-            h2_grouped[i] = g_h2
-
-        def quantise_h2(i):
-            h2_mx[i] = quantise(h2_grouped[i][:], ROUND_WIDTH, "h2")
-
-        def second_matmul(i):
+        def second_matmul(j):
             logits_ps = logits_pool.tile([P, R, CLASSES], F32, tag="logits_ps")
             for r in range(R):
-                operands = ((hh_mx[i], r * P), (hh_mx[i], (R + r) * P), (h2_mx[i], r * P))
+                operands = (
+                    (hh_mx[j], r * P),
+                    (hh_mx[j], (R + r) * P),
+                    (uq_mx[j], (R + r) * P),
+                )
                 for g in range(GROUPS):
                     (codes, scales), first = operands[g]
                     nodes = slice(first, first + P)
@@ -225,24 +249,30 @@ def tile_gin_pc_t_kernel(
                         start=(g == 0),
                         stop=(g == GROUPS - 1),
                     )
-            logits_bank[i] = logits_ps
+            logits_bank[j] = logits_ps
 
-        def add_b_out(i):
+        def add_b_out(j):
             nc.vector.tensor_tensor(
-                out=z_all[:, i * R : (i + 1) * R, :],
-                in0=logits_bank[i][:],
+                out=z_all[:, j * R : (j + 1) * R, :],
+                in0=logits_bank[j][:],
                 in1=bout_sb[:].unsqueeze(1).to_broadcast([P, R, CLASSES]),
                 op=ALU.add,
             )
 
-        def row_maximum(i):
-            tiles = slice(i * R, (i + 1) * R)
+        def row_maximum(j):
+            tiles = slice(j * R, (j + 1) * R)
             nc.vector.tensor_reduce(
                 out=neg_max[:, tiles], in_=z_all[:, tiles, :], axis=AXIS.X, op=ALU.max, negate=True
             )
 
-        def exponentials(i):
-            for t in range(i * R, (i + 1) * R):
+        def block_of(j):
+            if j + 1 in BLOCK_ENDS:
+                k = BLOCK_ENDS.index(j + 1)
+                return (BLOCK_ENDS[k - 1] if k else 0, j + 1)
+            return None
+
+        def exponentials(j):
+            for t in range(j * R, (j + 1) * R):
                 exp_sb = scratch.tile([P, CLASSES], F32, tag="exp")
                 nc.scalar.activation(
                     out=exp_sb[:],
@@ -252,62 +282,80 @@ def tile_gin_pc_t_kernel(
                     scale=1.0,
                     accum_out=sum_exp[:, t : t + 1],
                 )
-            if (i + 1) % BLOCK_ROUNDS == 0:
-                block = slice((i + 1 - BLOCK_ROUNDS) * R, (i + 1) * R)
+            if block_of(j):
+                first, end = block_of(j)
+                block = slice(first * R, end * R)
                 nc.scalar.activation(out=log_sum[:, block], in_=sum_exp[:, block], func=ACT.Ln)
 
-        def block_total(i):
-            if (i + 1) % BLOCK_ROUNDS == 0:
-                block = slice((i + 1 - BLOCK_ROUNDS) * R, (i + 1) * R)
+        scalar_todo, vector_todo = [], []
+
+        def block_total(j):
+            if block_of(j):
+                first, end = block_of(j)
+                block = slice(first * R, end * R)
                 nc.vector.tensor_tensor(
                     out=neg_total[:, block],
                     in0=neg_max[:, block],
                     in1=log_sum[:, block],
                     op=ALU.subtract,
                 )
+                tiles = list(range(first * R, end * R))
+                if end == BLOCK_ENDS[0]:
+                    scalar_todo.extend(tiles)
+                else:
+                    half = len(tiles) // 2
+                    scalar_todo.extend(tiles[:half])
+                    vector_todo.extend(tiles[half:])
 
-        def finish_first_tile(i):
-            t = i * R
-            nc.scalar.activation(
-                out=z_all[:, t, :],
-                in_=z_all[:, t, :],
-                func=ACT.Identity,
-                bias=neg_total[:, t : t + 1],
-                scale=1.0,
-            )
+        def store(first):
+            done = slice(first, first + LOAD_TILES)
+            nc.sync.dma_start(out=out_rows[:, done, :], in_=z_all[:, done, :])
 
-        def finish_second_tile_and_store(i):
-            t = i * R + 1
-            nc.vector.tensor_scalar_add(
-                out=z_all[:, t, :], in0=z_all[:, t, :], scalar1=neg_total[:, t : t + 1]
-            )
-            if (i + 1) % LOAD_ROUNDS == 0:
-                done = slice((i + 1) * R - LOAD_TILES, (i + 1) * R)
-                nc.sync.dma_start(out=out_rows[:, done, :], in_=z_all[:, done, :])
+        def finish_on_scalar(count):
+            for t in scalar_todo[:count]:
+                nc.scalar.activation(
+                    out=z_all[:, t, :],
+                    in_=z_all[:, t, :],
+                    func=ACT.Identity,
+                    bias=neg_total[:, t : t + 1],
+                    scale=1.0,
+                )
+                if (t + 1) % LOAD_TILES == 0:
+                    store(t + 1 - LOAD_TILES)
+            scalar_todo[:count] = []
 
-        def prefetch(step):
-            chunk = step // LOAD_ROUNDS + X_BUFS - 1
-            if step >= LOAD_ROUNDS and step % LOAD_ROUNDS == 0 and chunk < CHUNKS:
-                load_chunk(chunk)
+        def finish_on_vector():
+            while vector_todo:
+                first = vector_todo[0]
+                tiles = slice(first, first + LOAD_TILES)
+                nc.vector.tensor_tensor(
+                    out=z_all[:, tiles, :],
+                    in0=z_all[:, tiles, :],
+                    in1=neg_total[:, tiles].unsqueeze(2).to_broadcast([P, LOAD_TILES, CLASSES]),
+                    op=ALU.add,
+                )
+                store(first)
+                vector_todo[:LOAD_TILES] = []
 
-        def if_live(stage, i):
-            if 0 <= i < ROUNDS:
-                stage(i)
+        def if_live(stage, j, first=0):
+            if first <= j < UNITS:
+                stage(j)
 
-        for step in range(ROUNDS + LAG_FINISH):
-            prefetch(step)
-            if_live(quantise_h2, step - LAG_LOGITS)
-            if_live(add_b2_1, step - LAG_H2)
-            if_live(turn_u1_and_h, step)
-            if_live(second_matmul, step - LAG_LOGITS)
-            if_live(exponentials, step - LAG_EXP)
-            if_live(finish_first_tile, step - LAG_FINISH)
-            if_live(turn_h1, step)
-            if_live(turn_h2, step - LAG_H2)
-            if_live(quantise_u1, step)
-            if_live(first_matmul, step)
-            if_live(add_b_out, step - LAG_MAXIMUM)
-            if_live(quantise_h_and_h1, step - LAG_H2)
-            if_live(row_maximum, step - LAG_MAXIMUM)
-            if_live(block_total, step - LAG_EXP)
-            if_live(finish_second_tile_and_store, step - LAG_FINISH)
+        last_step = UNITS - 1 + LAG_EXP + 1
+        for s in range(-LEAD_TU, last_step + 1):
+            draining = s >= UNITS
+            if_live(quantise_uq, s, first=-1)
+            if_live(second_matmul, s - LAG_MM2)
+            if_live(first_matmul, s + 1)
+            if_live(add_b_out, s - LAG_Z)
+            if_live(quantise_hh, s)
+            if_live(exponentials, s - LAG_EXP)
+            finish_on_scalar(4 if draining else FIN_PER_STEP)
+            if_live(add_b2_1, s + 1)
+            if_live(row_maximum, s - LAG_Z)
+            if_live(block_total, s - LAG_EXP - 1)
+            if s - LAG_Z >= UNITS - 1:
+                finish_on_vector()
+            if_live(turn_u1, s + LEAD_TU)
+            if_live(turn_h_and_h1, s + LEAD_TH)
+        finish_on_scalar(len(scalar_todo))

@@ -34,7 +34,8 @@ X_BUFS = 4
 BLOCK_ENDS = (16, 28, 32)
 FIN_PER_STEP = 3
 
-LEAD_TU = 3
+LEAD_TU = 4
+U_AHEAD = 2
 LEAD_TH = 2
 LAG_MM2 = 1
 LAG_Z = 2
@@ -65,16 +66,19 @@ def tile_gin_pc_t_kernel(
 
         u1_sb, h_sb, h1_sb = {}, {}, {}
 
-        def load_rows(rows, store, chunk, tag, pieces=1):
+        def load_rows(rows, store, chunk, tag):
             x_sb = x_pool.tile([P, LOAD_TILES, HID], BF16, tag=tag)
-            step = LOAD_TILES // pieces
-            for piece in range(pieces):
-                lo = piece * step
-                nc.sync.dma_start(
-                    out=x_sb[:, lo : lo + step, :],
-                    in_=rows[:, chunk * LOAD_TILES + lo : chunk * LOAD_TILES + lo + step, :],
-                )
+            tiles = slice(chunk * LOAD_TILES, (chunk + 1) * LOAD_TILES)
+            nc.sync.dma_start(out=x_sb[:], in_=rows[:, tiles, :])
             store[chunk] = x_sb
+
+        def load_unit(rows, store, j, tag):
+            if j % LOAD_UNITS == 0:
+                store[j // LOAD_UNITS] = x_pool.tile([P, LOAD_TILES, HID], BF16, tag=tag, name=tag)
+            lo = (j % LOAD_UNITS) * R
+            nc.sync.dma_start(
+                out=store[j // LOAD_UNITS][:, lo : lo + R, :], in_=rows[:, j * R : (j + 1) * R, :]
+            )
 
         w21_scales_raw = consts.tile([P, HID], U8, align_bytes=64)
         wout_scales = consts.tile([P, GROUPS, CLASSES], U8, align_bytes=64)
@@ -89,7 +93,7 @@ def tile_gin_pc_t_kernel(
         bout_sb = consts.tile([P, CLASSES], BF16)
         nc.scalar.dma_start(out=bout_sb[:], in_=b_out.partition_broadcast(P))
 
-        load_rows(u1_rows, u1_sb, 0, "u1", pieces=2)
+        load_unit(u1_rows, u1_sb, 0, "u1")
         w21_words_raw = consts.tile([P, HID], U32, align_bytes=64)
         nc.sync.dma_start(
             out=w21_words_raw[:].bitcast(I32),
@@ -100,8 +104,13 @@ def tile_gin_pc_t_kernel(
                 out=w21_scales_raw[32 * quadrant : 32 * quadrant + 4, :].bitcast(I32),
                 in_=W2_1_scales[0, 4 * quadrant : 4 * quadrant + 4, :].bitcast(I32),
             )
-        load_rows(h_rows, h_sb, 0, "h", pieces=2)
-        load_rows(h1_rows, h1_sb, 0, "h1", pieces=2)
+        load_unit(u1_rows, u1_sb, 1, "u1")
+        load_unit(u1_rows, u1_sb, 2, "u1")
+        load_unit(h_rows, h_sb, 0, "h")
+        load_unit(h1_rows, h1_sb, 0, "h1")
+        load_unit(u1_rows, u1_sb, 3, "u1")
+        load_unit(h_rows, h_sb, 1, "h")
+        load_unit(h1_rows, h1_sb, 1, "h1")
         wout_words = consts.tile([P, GROUPS, CLASSES], U32, align_bytes=64)
         nc.sync.dma_start(
             out=wout_words[:].bitcast(I32),
@@ -115,7 +124,8 @@ def tile_gin_pc_t_kernel(
                 .bitcast(I32),
             )
         for chunk in range(1, X_BUFS):
-            load_rows(u1_rows, u1_sb, chunk, "u1")
+            if chunk > 1:
+                load_rows(u1_rows, u1_sb, chunk, "u1")
             load_rows(h_rows, h_sb, chunk, "h")
             load_rows(h1_rows, h1_sb, chunk, "h1")
 
@@ -165,7 +175,7 @@ def tile_gin_pc_t_kernel(
                 load_rows(rows, store, chunk, tag)
 
         def turn_u1(j):
-            turn_and_regroup(u1_sb, j, uq_tile(j - 1)[:, 0, :])
+            turn_and_regroup(u1_sb, j, uq_tile(j - U_AHEAD)[:, 0, :])
             refill(u1_rows, u1_sb, j, "u1")
 
         def turn_h_and_h1(j):
@@ -179,7 +189,7 @@ def tile_gin_pc_t_kernel(
         def quantise_uq(j):
             codes = codes_pool.tile([P, 2 * UNIT_CODES], U32, tag="uq_codes", align_bytes=64)
             scales = codes_pool.tile([P, 2 * UNIT_CODES], U8, tag="uq_scales", align_bytes=64)
-            lo = 0 if j + 1 < UNITS else 1
+            lo = 0 if j + U_AHEAD < UNITS else 1
             hi = 2 if j >= 0 else 1
             nc.vector.quantize_mx(
                 out=codes[:, lo * UNIT_CODES : hi * UNIT_CODES].bitcast(FP8X4),
@@ -199,7 +209,7 @@ def tile_gin_pc_t_kernel(
             hh_mx[j] = (codes, scales)
 
         def first_matmul(j):
-            codes, scales = uq_mx[j - 1]
+            codes, scales = uq_mx[j - U_AHEAD]
             h2_banks[j] = []
             for r in range(R):
                 nodes = slice(r * P, (r + 1) * P)
@@ -344,9 +354,9 @@ def tile_gin_pc_t_kernel(
         last_step = UNITS - 1 + LAG_EXP + 1
         for s in range(-LEAD_TU, last_step + 1):
             draining = s >= UNITS
-            if_live(quantise_uq, s, first=-1)
             if_live(second_matmul, s - LAG_MM2)
             if_live(first_matmul, s + 1)
+            if_live(quantise_uq, s, first=-U_AHEAD)
             if_live(add_b_out, s - LAG_Z)
             if_live(quantise_hh, s)
             if_live(exponentials, s - LAG_EXP)

@@ -262,9 +262,11 @@ def tile_gin_pc_t_kernel(
             logits_bank[j] = logits_ps
 
         def add_b_out(j):
-            nc.vector.tensor_tensor(
-                out=z_all[:, j * R : (j + 1) * R, :],
-                in0=logits_bank[j][:],
+            tiles = slice(j * R, (j + 1) * R)
+            nc.scalar.copy(out=z_all[:, tiles, :], in_=logits_bank[j][:])
+            nc.gpsimd.tensor_tensor(
+                out=z_all[:, tiles, :],
+                in0=z_all[:, tiles, :],
                 in1=bout_sb[:].unsqueeze(1).to_broadcast([P, R, CLASSES]),
                 op=ALU.add,
             )
@@ -297,7 +299,7 @@ def tile_gin_pc_t_kernel(
                 block = slice(first * R, end * R)
                 nc.scalar.activation(out=log_sum[:, block], in_=sum_exp[:, block], func=ACT.Ln)
 
-        scalar_todo, vector_todo = [], []
+        gpsimd_todo, scalar_todo, vector_todo = [], [], []
 
         def block_total(j):
             if block_of(j):
@@ -311,7 +313,7 @@ def tile_gin_pc_t_kernel(
                 )
                 tiles = list(range(first * R, end * R))
                 if end == BLOCK_ENDS[0]:
-                    scalar_todo.extend(tiles)
+                    gpsimd_todo.extend(tiles)
                 else:
                     half = len(tiles) // 2
                     scalar_todo.extend(tiles[:half])
@@ -333,6 +335,20 @@ def tile_gin_pc_t_kernel(
                 if (t + 1) % LOAD_TILES == 0:
                     store(t + 1 - LOAD_TILES)
             scalar_todo[:count] = []
+
+        def finish_on_gpsimd(count):
+            for t in gpsimd_todo[:count]:
+                nc.gpsimd.tensor_scalar(
+                    out=z_all[:, t, :],
+                    in0=z_all[:, t, :],
+                    scalar1=neg_total[:, t : t + 1],
+                    scalar2=1.0,
+                    op0=ALU.add,
+                    op1=ALU.mult,
+                )
+                if (t + 1) % LOAD_TILES == 0:
+                    store(t + 1 - LOAD_TILES)
+            gpsimd_todo[:count] = []
 
         def finish_on_vector():
             while vector_todo:
@@ -357,9 +373,10 @@ def tile_gin_pc_t_kernel(
             if_live(second_matmul, s - LAG_MM2)
             if_live(first_matmul, s + 1)
             if_live(quantise_uq, s, first=-U_AHEAD)
-            if_live(add_b_out, s - LAG_Z)
             if_live(quantise_hh, s)
             if_live(exponentials, s - LAG_EXP)
+            if_live(add_b_out, s - LAG_MM2)
+            finish_on_gpsimd(FIN_PER_STEP)
             finish_on_scalar(4 if draining else FIN_PER_STEP)
             if_live(add_b2_1, s + 1)
             if_live(row_maximum, s - LAG_Z)

from contextlib import ExitStack

import concourse.mybir as mybir
from concourse.masks import make_identity

F32 = mybir.dt.float32
BF16 = mybir.dt.bfloat16
I32 = mybir.dt.int32
U32 = mybir.dt.uint32
U8 = mybir.dt.uint8
FP8X4 = mybir.dt.float8_e4m3fn_x4
ALU = mybir.AluOpType
ACT = mybir.ActivationFunctionType
AXIS = mybir.AxisListType

P = 128
NODES = 8192
HID = 512
CLASSES = 128
GROUPS = 3
PACK = 4
WORDS = HID // 2

ROW_TILES = NODES // P
R = 2
UNITS = ROW_TILES // R
UNIT_WIDTH = R * P * PACK
UNIT_CODES = R * P
LOAD_TILES = 4
LOAD_UNITS = LOAD_TILES // R
CHUNKS = ROW_TILES // LOAD_TILES
X_BUFS = 4

BLOCK_ENDS = (16, 28, 32)
FIN_PER_STEP = 3

LEAD_TU = 4
U_AHEAD = 2
LEAD_TH = 2
LAG_MM2 = 1
LAG_Z = 2
LAG_EXP = 3

FLOPS = 2 * NODES * HID * HID + 2 * NODES * GROUPS * HID * CLASSES


def tile_gin_pc_t_kernel(
    tc, u1, W2_1_words, W2_1_scales, b2_1, h, h1, W_out_words, W_out_scales, b_out, out
):
    nc = tc.nc
    with ExitStack() as ctx:
        ctx.enter_context(tc.manual_schedule())
        consts = ctx.enter_context(tc.tile_pool(name="consts", bufs=1))
        x_pool = ctx.enter_context(tc.tile_pool(name="x", bufs=X_BUFS))
        grouped_pool = ctx.enter_context(tc.tile_pool(name="grouped", bufs=4))
        codes_pool = ctx.enter_context(tc.tile_pool(name="codes", bufs=3))
        scratch = ctx.enter_context(tc.tile_pool(name="scratch", bufs=4))
        turned_pool = ctx.enter_context(tc.psum_pool(name="turned", bufs=4))
        h2_pool = ctx.enter_context(tc.psum_pool(name="h2", bufs=2))
        logits_pool = ctx.enter_context(tc.psum_pool(name="logits", bufs=2))

        u1_rows = u1.rearrange("(p i) k -> p i k", i=ROW_TILES)
        h_rows = h.rearrange("(p i) k -> p i k", i=ROW_TILES)
        h1_rows = h1.rearrange("(p i) k -> p i k", i=ROW_TILES)
        out_rows = out.rearrange("(p i) c -> p i c", i=ROW_TILES)

        u1_sb, h_sb, h1_sb = {}, {}, {}

        def load_rows(rows, store, chunk, tag):
            x_sb = x_pool.tile([P, LOAD_TILES, HID], BF16, tag=tag)
            tiles = slice(chunk * LOAD_TILES, (chunk + 1) * LOAD_TILES)
            nc.sync.dma_start(out=x_sb[:], in_=rows[:, tiles, :])
            store[chunk] = x_sb

        def load_unit(rows, store, j, tag):
            if j % LOAD_UNITS == 0:
                store[j // LOAD_UNITS] = x_pool.tile([P, LOAD_TILES, HID], BF16, tag=tag, name=tag)
            lo = (j % LOAD_UNITS) * R
            nc.sync.dma_start(
                out=store[j // LOAD_UNITS][:, lo : lo + R, :], in_=rows[:, j * R : (j + 1) * R, :]
            )

        w21_scales_raw = consts.tile([P, HID], U8, align_bytes=64)
        wout_scales = consts.tile([P, GROUPS, CLASSES], U8, align_bytes=64)
        nc.vector.memset(w21_scales_raw[:].bitcast(I32), 0)
        nc.vector.memset(wout_scales[:].bitcast(I32), 0)

        ident = consts.tile([P, P], F32)
        make_identity(nc, ident[:])

        b21_sb = consts.tile([P, PACK], BF16)
        nc.scalar.dma_start(out=b21_sb[:], in_=b2_1.rearrange("(p t) -> p t", t=PACK))
        bout_sb = consts.tile([P, CLASSES], BF16)
        nc.scalar.dma_start(out=bout_sb[:], in_=b_out.partition_broadcast(P))

        load_unit(u1_rows, u1_sb, 0, "u1")
        w21_words_raw = consts.tile([P, HID], U32, align_bytes=64)
        nc.sync.dma_start(
            out=w21_words_raw[:].bitcast(I32),
            in_=W2_1_words[0].rearrange("p n t -> p (n t)").bitcast(I32),
        )
        for quadrant in range(4):
            nc.sync.dma_start(
                out=w21_scales_raw[32 * quadrant : 32 * quadrant + 4, :].bitcast(I32),
                in_=W2_1_scales[0, 4 * quadrant : 4 * quadrant + 4, :].bitcast(I32),
            )
        load_unit(u1_rows, u1_sb, 1, "u1")
        load_unit(u1_rows, u1_sb, 2, "u1")
        load_unit(h_rows, h_sb, 0, "h")
        load_unit(h1_rows, h1_sb, 0, "h1")
        load_unit(u1_rows, u1_sb, 3, "u1")
        load_unit(h_rows, h_sb, 1, "h")
        load_unit(h1_rows, h1_sb, 1, "h1")
        wout_words = consts.tile([P, GROUPS, CLASSES], U32, align_bytes=64)
        nc.sync.dma_start(
            out=wout_words[:].bitcast(I32),
            in_=W_out_words.rearrange("g p n t -> p g (n t)").bitcast(I32),
        )
        for quadrant in range(4):
            nc.sync.dma_start(
                out=wout_scales[32 * quadrant : 32 * quadrant + 4, :, :].bitcast(I32),
                in_=W_out_scales[:, 4 * quadrant : 4 * quadrant + 4, :]
                .rearrange("g r n -> r g n")
                .bitcast(I32),
            )
        for chunk in range(1, X_BUFS):
            if chunk > 1:
                load_rows(u1_rows, u1_sb, chunk, "u1")
            load_rows(h_rows, h_sb, chunk, "h")
            load_rows(h1_rows, h1_sb, chunk, "h1")

        w21_words = consts.tile([P, HID], U32, align_bytes=64)
        nc.vector.tensor_copy(
            out=w21_words[:].bitcast(I32).rearrange("p (t m) -> p t m", t=PACK),
            in_=w21_words_raw[:].bitcast(I32).rearrange("p (m t) -> p t m", t=PACK),
        )
        w21_scales = consts.tile([P, HID], U8, align_bytes=64)
        for t in range(PACK):
            nc.vector.tensor_copy(
                out=w21_scales[:, t * P : (t + 1) * P], in_=w21_scales_raw[:, t:HID:PACK]
            )

        z_all = consts.tile([P, ROW_TILES, CLASSES], F32)
        neg_max = consts.tile([P, ROW_TILES], F32)
        sum_exp = consts.tile([P, ROW_TILES], F32)
        log_sum = consts.tile([P, ROW_TILES], F32)
        neg_total = consts.tile([P, ROW_TILES], F32)

        uq_grouped, hh_grouped = {}, {}
        uq_mx, hh_mx = {}, {}
        h2_banks, logits_bank = {}, {}

        def uq_tile(j):
            if j not in uq_grouped:
                uq_grouped[j] = grouped_pool.tile(
                    [P, 2, UNIT_WIDTH], BF16, tag="uq_grouped", align_bytes=64, name="uq_g"
                )
            return uq_grouped[j]

        def turn_and_regroup(x_sb, j, grouped):
            words = x_sb[j // LOAD_UNITS][:].bitcast(F32)
            first = (j % LOAD_UNITS) * R
            bank = turned_pool.tile([P, R, 2, P], F32, tag="turned")
            for r in range(R):
                for u in range(2):
                    nc.tensor.transpose(bank[:, r, u, :], words[:, first + r, u:WORDS:2], ident[:])
            nc.scalar.copy(
                out=grouped.bitcast(F32).rearrange("p (r c u) -> p r c u", r=R, u=2),
                in_=bank[:].rearrange("p r u c -> p r c u"),
            )

        def refill(rows, store, j, tag):
            chunk = j // LOAD_UNITS + X_BUFS
            if j % LOAD_UNITS == LOAD_UNITS - 1 and chunk < CHUNKS:
                load_rows(rows, store, chunk, tag)

        def turn_u1(j):
            turn_and_regroup(u1_sb, j, uq_tile(j - U_AHEAD)[:, 0, :])
            refill(u1_rows, u1_sb, j, "u1")

        def turn_h_and_h1(j):
            g_hh = grouped_pool.tile([P, 2, UNIT_WIDTH], BF16, tag="hh_grouped", align_bytes=64)
            hh_grouped[j] = g_hh
            turn_and_regroup(h_sb, j, g_hh[:, 0, :])
            refill(h_rows, h_sb, j, "h")
            turn_and_regroup(h1_sb, j, g_hh[:, 1, :])
            refill(h1_rows, h1_sb, j, "h1")

        def quantise_uq(j):
            codes = codes_pool.tile([P, 2 * UNIT_CODES], U32, tag="uq_codes", align_bytes=64)
            scales = codes_pool.tile([P, 2 * UNIT_CODES], U8, tag="uq_scales", align_bytes=64)
            lo = 0 if j + U_AHEAD < UNITS else 1
            hi = 2 if j >= 0 else 1
            nc.vector.quantize_mx(
                out=codes[:, lo * UNIT_CODES : hi * UNIT_CODES].bitcast(FP8X4),
                scales=scales[:, lo * UNIT_CODES : hi * UNIT_CODES],
                in_=uq_tile(j)[:, lo:hi, :].rearrange("p s w -> p (s w)"),
            )
            uq_mx[j] = (codes, scales)

        def quantise_hh(j):
            codes = codes_pool.tile([P, 2 * UNIT_CODES], U32, tag="hh_codes", align_bytes=64)
            scales = codes_pool.tile([P, 2 * UNIT_CODES], U8, tag="hh_scales", align_bytes=64)
            nc.vector.quantize_mx(
                out=codes[:].bitcast(FP8X4),
                scales=scales[:],
                in_=hh_grouped[j][:].rearrange("p s w -> p (s w)"),
            )
            hh_mx[j] = (codes, scales)

        def first_matmul(j):
            codes, scales = uq_mx[j - U_AHEAD]
            h2_banks[j] = []
            for r in range(R):
                nodes = slice(r * P, (r + 1) * P)
                h2_ps = h2_pool.tile([P, PACK, P], F32, tag="h2_ps")
                for t in range(PACK):
                    channels = slice(t * P, (t + 1) * P)
                    nc.tensor.matmul_mx(
                        out=h2_ps[:, t, :],
                        lhsT=w21_words[:, channels].bitcast(FP8X4),
                        lhsT_scale=w21_scales[:, channels],
                        rhs=codes[:, nodes].bitcast(FP8X4),
                        rhs_scale=scales[:, nodes],
                        start=True,
                        stop=True,
                    )
                h2_banks[j].append(h2_ps)

        def add_b2_1(j):
            g = uq_tile(j)
            for r in range(R):
                nc.vector.tensor_tensor(
                    out=g[:, 1, r * P * PACK : (r + 1) * P * PACK].rearrange(
                        "p (c t) -> p c t", t=PACK
                    ),
                    in0=h2_banks[j][r][:].rearrange("p t c -> p c t"),
                    in1=b21_sb[:].unsqueeze(1).to_broadcast([P, P, PACK]),
                    op=ALU.add,
                )

        def second_matmul(j):
            logits_ps = logits_pool.tile([P, R, CLASSES], F32, tag="logits_ps")
            for r in range(R):
                operands = (
                    (hh_mx[j], r * P),
                    (hh_mx[j], (R + r) * P),
                    (uq_mx[j], (R + r) * P),
                )
                for g in range(GROUPS):
                    (codes, scales), first = operands[g]
                    nodes = slice(first, first + P)
                    nc.tensor.matmul_mx(
                        out=logits_ps[:, r, :],
                        lhsT=codes[:, nodes].bitcast(FP8X4),
                        lhsT_scale=scales[:, nodes],
                        rhs=wout_words[:, g, :].bitcast(FP8X4),
                        rhs_scale=wout_scales[:, g, :],
                        start=(g == 0),
                        stop=(g == GROUPS - 1),
                    )
            logits_bank[j] = logits_ps

        def add_b_out(j):
            tiles = slice(j * R, (j + 1) * R)
            nc.scalar.copy(out=z_all[:, tiles, :], in_=logits_bank[j][:])
            nc.gpsimd.tensor_tensor(
                out=z_all[:, tiles, :],
                in0=z_all[:, tiles, :],
                in1=bout_sb[:].unsqueeze(1).to_broadcast([P, R, CLASSES]),
                op=ALU.add,
            )

        def row_maximum(j):
            tiles = slice(j * R, (j + 1) * R)
            nc.vector.tensor_reduce(
                out=neg_max[:, tiles], in_=z_all[:, tiles, :], axis=AXIS.X, op=ALU.max, negate=True
            )

        def block_of(j):
            if j + 1 in BLOCK_ENDS:
                k = BLOCK_ENDS.index(j + 1)
                return (BLOCK_ENDS[k - 1] if k else 0, j + 1)
            return None

        def exponentials(j):
            for t in range(j * R, (j + 1) * R):
                exp_sb = scratch.tile([P, CLASSES], F32, tag="exp")
                nc.scalar.activation(
                    out=exp_sb[:],
                    in_=z_all[:, t, :],
                    func=ACT.Exp,
                    bias=neg_max[:, t : t + 1],
                    scale=1.0,
                    accum_out=sum_exp[:, t : t + 1],
                )
            if block_of(j):
                first, end = block_of(j)
                block = slice(first * R, end * R)
                nc.scalar.activation(out=log_sum[:, block], in_=sum_exp[:, block], func=ACT.Ln)

        gpsimd_todo, scalar_todo, vector_todo = [], [], []

        def block_total(j):
            if block_of(j):
                first, end = block_of(j)
                block = slice(first * R, end * R)
                nc.vector.tensor_tensor(
                    out=neg_total[:, block],
                    in0=neg_max[:, block],
                    in1=log_sum[:, block],
                    op=ALU.subtract,
                )
                tiles = list(range(first * R, end * R))
                if end == BLOCK_ENDS[0]:
                    gpsimd_todo.extend(tiles)
                else:
                    half = len(tiles) // 2
                    scalar_todo.extend(tiles[:half])
                    vector_todo.extend(tiles[half:])

        def store(first):
            done = slice(first, first + LOAD_TILES)
            nc.sync.dma_start(out=out_rows[:, done, :], in_=z_all[:, done, :])

        def finish_on_scalar(count):
            for t in scalar_todo[:count]:
                nc.scalar.activation(
                    out=z_all[:, t, :],
                    in_=z_all[:, t, :],
                    func=ACT.Identity,
                    bias=neg_total[:, t : t + 1],
                    scale=1.0,
                )
                if (t + 1) % LOAD_TILES == 0:
                    store(t + 1 - LOAD_TILES)
            scalar_todo[:count] = []

        def finish_on_gpsimd(count):
            for t in gpsimd_todo[:count]:
                nc.gpsimd.tensor_scalar(
                    out=z_all[:, t, :],
                    in0=z_all[:, t, :],
                    scalar1=neg_total[:, t : t + 1],
                    scalar2=1.0,
                    op0=ALU.add,
                    op1=ALU.mult,
                )
                if (t + 1) % LOAD_TILES == 0:
                    store(t + 1 - LOAD_TILES)
            gpsimd_todo[:count] = []

        def finish_on_vector():
            while vector_todo:
                first = vector_todo[0]
                tiles = slice(first, first + LOAD_TILES)
                nc.vector.tensor_tensor(
                    out=z_all[:, tiles, :],
                    in0=z_all[:, tiles, :],
                    in1=neg_total[:, tiles].unsqueeze(2).to_broadcast([P, LOAD_TILES, CLASSES]),
                    op=ALU.add,
                )
                store(first)
                vector_todo[:LOAD_TILES] = []

        def if_live(stage, j, first=0):
            if first <= j < UNITS:
                stage(j)

        last_step = UNITS - 1 + LAG_EXP + 1
        for s in range(-LEAD_TU, last_step + 1):
            draining = s >= UNITS
            if_live(second_matmul, s - LAG_MM2)
            if_live(first_matmul, s + 1)
            if_live(quantise_uq, s, first=-U_AHEAD)
            if_live(quantise_hh, s)
            if_live(exponentials, s - LAG_EXP)
            if_live(add_b_out, s - LAG_MM2)
            finish_on_gpsimd(FIN_PER_STEP)
            finish_on_scalar(4 if draining else FIN_PER_STEP)
            if_live(add_b2_1, s + 1)
            if_live(row_maximum, s - LAG_Z)
            if_live(block_total, s - LAG_EXP - 1)
            if s - LAG_Z >= UNITS - 1:
                finish_on_vector()
            if_live(turn_u1, s + LEAD_TU)
            if_live(turn_h_and_h1, s + LEAD_TH)
        finish_on_scalar(len(scalar_todo))
